import numpy as np
import ml_dtypes


def mxq(x, axis, fmt="e4m3"):
    dtype, down = {"e4m3": (ml_dtypes.float8_e4m3fn, 7), "e5m2": (ml_dtypes.float8_e5m2, 14)}[fmt]
    v = np.moveaxis(np.asarray(x, np.float32).astype(ml_dtypes.bfloat16).astype(np.float64), axis, -1)
    blocks = v.reshape(v.shape[:-1] + (-1, 32))
    amax = np.abs(blocks).max(-1, keepdims=True)
    byte = np.maximum(np.where(amax > 0, np.frexp(amax)[1] - 1 + 127, 0) - down, 1)
    scale = np.exp2(byte - 127.0)
    codes = (blocks / scale).astype(np.float32).astype(dtype).astype(np.float64)
    return np.moveaxis((codes * scale).reshape(v.shape), -1, axis)


WIDE = False


def mx_kscale(k):
    if not WIDE:
        return np.ones(k)
    levels = np.array([10, -10, 5, -5, 0])
    a = np.random.permutation(np.resize(levels, k // 512 * 4)).reshape(k // 512, 4)
    idx = np.arange(k)
    return np.exp2(a[idx // 512, idx % 128 // 32])


BF16 = ml_dtypes.bfloat16


def bf(x):
    return np.asarray(x, np.float32).astype(BF16)


def f64(x):
    return np.asarray(x).astype(np.float64)


B, T, D, H, DH, DFF = 4, 256, 1024, 16, 64, 4096
HD = H * DH
EPS = 1e-5


def layer_norm(x, w):
    mu = x.mean(-1, keepdims=True)
    var = ((x - mu) ** 2).mean(-1, keepdims=True)
    return (x - mu) * (1.0 / np.sqrt(var + EPS)) * w


def setup_inputs():
    s = mx_kscale(D)
    spread = 0.5 + np.random.random((B, T, 1))
    shift = 0.5 * np.random.standard_normal((B, T, 1))
    return {"x": bf(np.random.standard_normal((B, T, D)) * spread + shift),
            "ln1_w": bf((1.0 + 0.1 * np.random.standard_normal(D)) * s),
            "qkv_w": bf(np.random.standard_normal((3 * HD, D)) / np.sqrt(D) / s[None, :])}


def reference(x, ln1_w, qkv_w):
    h = layer_norm(f64(x), f64(ln1_w))
    qkv = mxq(h, 2, "e4m3") @ mxq(f64(qkv_w), 1, "e4m3").T
    qkv = qkv.reshape(B, T, 3, H, DH)
    q = qkv[:, :, 0].transpose(0, 2, 1, 3)
    k = qkv[:, :, 1].transpose(0, 2, 1, 3)
    v = qkv[:, :, 2].transpose(0, 2, 1, 3)
    return q, k, v

@@ -1,0 +1,200 @@
+from contextlib import ExitStack
+
+import concourse.mybir as mybir
+from concourse.masks import make_identity
+
+F32 = mybir.dt.float32
+BF16 = mybir.dt.bfloat16
+U32 = mybir.dt.uint32
+U8 = mybir.dt.uint8
+FP8X4 = mybir.dt.float8_e4m3fn_x4
+ALU = mybir.AluOpType
+ACT = mybir.ActivationFunctionType
+
+P = 128
+BATCH, SEQ, DIM = 4, 256, 1024
+HEADS, HEAD_DIM = 16, 64
+EPS = 1e-5
+
+PACK = 4
+K_PASS = P * PACK
+PASSES = DIM // K_PASS
+SLOTS = BATCH * SEQ // P
+HALF = SLOTS // 2
+CHUNK = 512
+CHUNK_HEADS = CHUNK // HEAD_DIM
+CHUNKS = 3 * HEADS * HEAD_DIM // CHUNK
+ROW_BLOCKS = CHUNK // P
+BN_WIDTH = 512
+
+EARLY_CHUNKS = 3
+
+FLOPS = 2 * BATCH * SEQ * DIM * 3 * HEADS * HEAD_DIM
+
+
+def tile_traceableencoderlayer_pa_kernel(tc, x, ln1_w, qkv_w, out_0, out_1, out_2):
+    nc = tc.nc
+    outs = (out_0, out_1, out_2)
+
+    with ExitStack() as ctx:
+        keep = ctx.enter_context(tc.tile_pool(name="keep", bufs=1))
+        small = ctx.enter_context(tc.tile_pool(name="small", bufs=4))
+        stage = ctx.enter_context(tc.tile_pool(name="stage", bufs=2))
+        w_pool = ctx.enter_context(tc.tile_pool(name="w_pool", bufs=CHUNKS))
+        res_pool = ctx.enter_context(tc.tile_pool(name="res_pool", bufs=4))
+        flip_psum = ctx.enter_context(tc.psum_pool(name="flip_psum", bufs=4))
+        acc_psum = ctx.enter_context(tc.psum_pool(name="acc_psum", bufs=4))
+
+        x_sb = keep.tile([P, SLOTS, DIM], BF16)
+        for half in range(2):
+            slots = slice(half * HALF, (half + 1) * HALF)
+            for b in range(BATCH):
+                nc.sync.dma_start(
+                    out=x_sb[b:P:BATCH, slots, :],
+                    in_=x[b].rearrange("(i r) k -> i r k", r=SLOTS)[:, slots, :],
+                )
+        w_rows = qkv_w.rearrange("(c a p) k -> c p a k", a=ROW_BLOCKS, p=P)
+        w_raw = []
+        for c in range(CHUNKS):
+            raw = w_pool.tile([P, ROW_BLOCKS, DIM], BF16, name="raw")
+            nc.sync.dma_start(out=raw[:], in_=w_rows[c])
+            w_raw.append(raw)
+
+        identity = keep.tile([P, P], F32)
+        make_identity(nc, identity[:])
+
+        gain_rows = keep.tile([P, 2 * P], BF16)
+        nc.vector.memset(gain_rows[:], 0.0)
+        nc.scalar.dma_start(
+            out=gain_rows[0 : 2 * PASSES, :], in_=ln1_w.rearrange("(r c) -> r c", c=2 * P)
+        )
+        gain_flip = flip_psum.tile([P, PACK, P], F32, tag="flip")
+        nc.tensor.transpose(gain_flip[:, 0, :], gain_rows[:].bitcast(F32), identity[:])
+        gain_words = keep.tile([P, 2 * PASSES], F32)
+        nc.vector.tensor_copy(out=gain_words[:], in_=gain_flip[:, 0, 0 : 2 * PASSES])
+        gain = keep.tile([P, PASSES, PACK], F32)
+        nc.vector.tensor_copy(
+            out=gain[:].rearrange("p g j -> p (g j)"), in_=gain_words[:].bitcast(BF16)
+        )
+
+        minus_half = keep.tile([P, HALF], F32)
+        nc.gpsimd.memset(minus_half[:], -0.5)
+
+        mean_var = keep.tile([P, SLOTS, 2], F32)
+        neg_mean = keep.tile([P, SLOTS], F32)
+        var_eps = keep.tile([P, SLOTS], F32)
+        rstd = keep.tile([P, SLOTS], F32)
+        shift = keep.tile([P, SLOTS], F32)
+        h_codes = keep.tile([P, SLOTS, PASSES, P], U32, align_bytes=64)
+        h_scales = keep.tile([P, SLOTS, PASSES, P], U8, align_bytes=64)
+        w_codes = keep.tile([P, CHUNKS, PASSES, CHUNK], U32, align_bytes=64)
+        w_scales = keep.tile([P, CHUNKS, PASSES, CHUNK], U8, align_bytes=64)
+
+        def layer_norm_half(half):
+            slots = slice(half * HALF, (half + 1) * HALF)
+            for r in range(half * HALF, (half + 1) * HALF):
+                stats = small.tile([P, DIM // BN_WIDTH, 6], F32)
+                for s in range(DIM // BN_WIDTH):
+                    nc.vector.bn_stats(
+                        out=stats[:, s, :], in_=x_sb[:, r, s * BN_WIDTH : (s + 1) * BN_WIDTH]
+                    )
+                nc.vector.bn_aggr(out=mean_var[:, r, :], in_=stats[:].rearrange("p s f -> p (s f)"))
+            nc.vector.tensor_scalar_mul(out=neg_mean[:, slots], in0=mean_var[:, slots, 0], scalar1=-1.0)
+            nc.gpsimd.tensor_scalar_add(out=var_eps[:, slots], in0=mean_var[:, slots, 1], scalar1=EPS)
+            nc.gpsimd.tensor_tensor(
+                out=rstd[:, slots], in0=var_eps[:, slots], in1=minus_half[:], op=ALU.pow
+            )
+            nc.gpsimd.tensor_tensor(
+                out=shift[:, slots], in0=neg_mean[:, slots], in1=rstd[:, slots], op=ALU.mult
+            )
+            for r in range(half * HALF, (half + 1) * HALF):
+                z = stage.tile([P, 2 * PASSES, 2, P], F32, bufs=3)
+                nc.scalar.activation(
+                    out=z[:],
+                    in_=x_sb[:, r, :].rearrange("p (c w e) -> p c e w", w=P, e=2),
+                    func=ACT.Identity,
+                    scale=rstd[:, r : r + 1],
+                    bias=shift[:, r : r + 1],
+                )
+                h_grouped = stage.tile([P, PASSES, P, PACK], BF16, align_bytes=64)
+                for g in range(PASSES):
+                    z_flip = flip_psum.tile([P, PACK, P], F32, tag="flip")
+                    for j in range(PACK):
+                        nc.tensor.transpose(z_flip[:, j, :], z[:, 2 * g + j // 2, j % 2, :], identity[:])
+                    nc.vector.tensor_tensor(
+                        out=h_grouped[:, g, :, :],
+                        in0=z_flip[:].rearrange("p j i -> p i j"),
+                        in1=gain[:, g, :].unsqueeze(1).to_broadcast([P, P, PACK]),
+                        op=ALU.mult,
+                    )
+                nc.vector.quantize_mx(
+                    out=h_codes[:, r, :, :].rearrange("p g i -> p (g i)").bitcast(FP8X4),
+                    scales=h_scales[:, r, :, :].rearrange("p g i -> p (g i)"),
+                    in_=h_grouped[:].rearrange("p g i j -> p (g i j)"),
+                )
+
+        def quantise_weights(c):
+            words = w_raw[c][:].bitcast(F32)
+            w_grouped = stage.tile([P, PASSES, CHUNK, PACK], BF16, align_bytes=64)
+            grouped_words = w_grouped[:].bitcast(F32)
+            for g in range(PASSES):
+                for pair in range(ROW_BLOCKS // 2):
+                    w_flip = flip_psum.tile([P, 2, 2, P], F32, tag="flip")
+                    for u in range(2):
+                        for a in range(2):
+                            first = (2 * g + u) * P
+                            nc.tensor.transpose(
+                                w_flip[:, u, a, :],
+                                words[:, 2 * pair + a, first : first + P],
+                                identity[:],
+                            )
+                    nc.scalar.copy(
+                        out=grouped_words[:, g, 2 * pair * P : (2 * pair + 2) * P, :],
+                        in_=w_flip[:].rearrange("p u a n -> p (a n) u"),
+                    )
+            nc.vector.quantize_mx(
+                out=w_codes[:, c, :, :].rearrange("p g n -> p (g n)").bitcast(FP8X4),
+                scales=w_scales[:, c, :, :].rearrange("p g n -> p (g n)"),
+                in_=w_grouped[:].rearrange("p g n j -> p (g n j)"),
+            )
+
+        def project(c, first_slot, n_slots):
+            result = res_pool.tile([P, CHUNK_HEADS, n_slots, HEAD_DIM], F32, tag="result")
+            for r in range(first_slot, first_slot + n_slots):
+                acc = acc_psum.tile([P, CHUNK], F32)
+                for g in range(PASSES):
+                    nc.tensor.matmul_mx(
+                        out=acc[:],
+                        lhsT=h_codes[:, r, g, :].bitcast(FP8X4),
+                        lhsT_scale=h_scales[:, r, g, :],
+                        rhs=w_codes[:, c, g, :].bitcast(FP8X4),
+                        rhs_scale=w_scales[:, c, g, :],
+                        start=(g == 0),
+                        stop=(g == PASSES - 1),
+                    )
+                by_head = acc[:].rearrange("p (n d) -> p n d", d=HEAD_DIM)
+                if r % 2 == 1:
+                    nc.vector.tensor_copy(out=result[:, :, r - first_slot, :], in_=by_head)
+                else:
+                    nc.scalar.copy(out=result[:, :, r - first_slot, :], in_=by_head)
+            which, first_head = divmod(c * CHUNK_HEADS, HEADS)
+            for b in range(BATCH):
+                nc.sync.dma_start(
+                    out=outs[which][b, first_head : first_head + CHUNK_HEADS].rearrange(
+                        "n (i r) d -> i n r d", r=SLOTS
+                    )[:, :, first_slot : first_slot + n_slots, :],
+                    in_=result[b:P:BATCH],
+                )
+
+        layer_norm_half(0)
+        quantise_weights(0)
+        for c in range(EARLY_CHUNKS):
+            quantise_weights(c + 1)
+            project(c, 0, HALF)
+        layer_norm_half(1)
+        for c in range(EARLY_CHUNKS):
+            project(c, HALF, HALF)
+        for c in range(EARLY_CHUNKS, CHUNKS):
+            if c + 1 < CHUNKS:
+                quantise_weights(c + 1)
+            project(c, 0, SLOTS)

@@ -27,7 +27,7 @@ CHUNKS = 3 * HEADS * HEAD_DIM // CHUNK
 ROW_BLOCKS = CHUNK // P
 BN_WIDTH = 512
 
-EARLY_CHUNKS = 3
+EARLY_CHUNKS = HALF
 
 FLOPS = 2 * BATCH * SEQ * DIM * 3 * HEADS * HEAD_DIM
 
@@ -42,46 +42,56 @@ def tile_traceableencoderlayer_pa_kernel(tc, x, ln1_w, qkv_w, out_0, out_1, out_
         stage = ctx.enter_context(tc.tile_pool(name="stage", bufs=2))
         w_pool = ctx.enter_context(tc.tile_pool(name="w_pool", bufs=CHUNKS))
         res_pool = ctx.enter_context(tc.tile_pool(name="res_pool", bufs=4))
-        flip_psum = ctx.enter_context(tc.psum_pool(name="flip_psum", bufs=4))
-        acc_psum = ctx.enter_context(tc.psum_pool(name="acc_psum", bufs=4))
+        psum = ctx.enter_context(tc.psum_pool(name="psum", bufs=8))
+        ctx.enter_context(tc.manual_schedule())
 
         x_sb = keep.tile([P, SLOTS, DIM], BF16)
-        for half in range(2):
+        w_rows = qkv_w.rearrange("(c a p) k -> c p a k", a=ROW_BLOCKS, p=P)
+        w_raw = []
+
+        def load_tokens(half):
             slots = slice(half * HALF, (half + 1) * HALF)
             for b in range(BATCH):
                 nc.sync.dma_start(
                     out=x_sb[b:P:BATCH, slots, :],
                     in_=x[b].rearrange("(i r) k -> i r k", r=SLOTS)[:, slots, :],
                 )
-        w_rows = qkv_w.rearrange("(c a p) k -> c p a k", a=ROW_BLOCKS, p=P)
-        w_raw = []
-        for c in range(CHUNKS):
+
+        def load_weights(c):
             raw = w_pool.tile([P, ROW_BLOCKS, DIM], BF16, name="raw")
             nc.sync.dma_start(out=raw[:], in_=w_rows[c])
             w_raw.append(raw)
 
+        load_tokens(0)
+        load_weights(0)
+        load_tokens(1)
+        for c in range(1, CHUNKS):
+            load_weights(c)
+
         identity = keep.tile([P, P], F32)
         make_identity(nc, identity[:])
+        minus_half = keep.tile([P, 1], F32)
+        nc.gpsimd.memset(minus_half[:], -0.5)
+        table_warmer = keep.tile([P, 1], F32)
+        nc.scalar.activation(out=table_warmer[:], in_=minus_half[:], func=ACT.Identity)
 
         gain_rows = keep.tile([P, 2 * P], BF16)
         nc.vector.memset(gain_rows[:], 0.0)
         nc.scalar.dma_start(
             out=gain_rows[0 : 2 * PASSES, :], in_=ln1_w.rearrange("(r c) -> r c", c=2 * P)
         )
-        gain_flip = flip_psum.tile([P, PACK, P], F32, tag="flip")
+        gain_flip = psum.tile([P, PACK, P], F32, tag="bank")
         nc.tensor.transpose(gain_flip[:, 0, :], gain_rows[:].bitcast(F32), identity[:])
         gain_words = keep.tile([P, 2 * PASSES], F32)
-        nc.vector.tensor_copy(out=gain_words[:], in_=gain_flip[:, 0, 0 : 2 * PASSES])
         gain = keep.tile([P, PASSES, PACK], F32)
-        nc.vector.tensor_copy(
-            out=gain[:].rearrange("p g j -> p (g j)"), in_=gain_words[:].bitcast(BF16)
-        )
 
-        minus_half = keep.tile([P, HALF], F32)
-        nc.gpsimd.memset(minus_half[:], -0.5)
+        def widen_gain():
+            nc.vector.tensor_copy(out=gain_words[:], in_=gain_flip[:, 0, 0 : 2 * PASSES])
+            nc.vector.tensor_copy(
+                out=gain[:].rearrange("p g j -> p (g j)"), in_=gain_words[:].bitcast(BF16)
+            )
 
         mean_var = keep.tile([P, SLOTS, 2], F32)
-        neg_mean = keep.tile([P, SLOTS], F32)
         var_eps = keep.tile([P, SLOTS], F32)
         rstd = keep.tile([P, SLOTS], F32)
         shift = keep.tile([P, SLOTS], F32)
@@ -89,57 +99,71 @@ def tile_traceableencoderlayer_pa_kernel(tc, x, ln1_w, qkv_w, out_0, out_1, out_
         h_scales = keep.tile([P, SLOTS, PASSES, P], U8, align_bytes=64)
         w_codes = keep.tile([P, CHUNKS, PASSES, CHUNK], U32, align_bytes=64)
         w_scales = keep.tile([P, CHUNKS, PASSES, CHUNK], U8, align_bytes=64)
+        z_tiles = {}
+        h_grouped_tiles = {}
+        w_grouped_tiles = {}
 
-        def layer_norm_half(half):
-            slots = slice(half * HALF, (half + 1) * HALF)
-            for r in range(half * HALF, (half + 1) * HALF):
-                stats = small.tile([P, DIM // BN_WIDTH, 6], F32)
-                for s in range(DIM // BN_WIDTH):
-                    nc.vector.bn_stats(
-                        out=stats[:, s, :], in_=x_sb[:, r, s * BN_WIDTH : (s + 1) * BN_WIDTH]
-                    )
-                nc.vector.bn_aggr(out=mean_var[:, r, :], in_=stats[:].rearrange("p s f -> p (s f)"))
-            nc.vector.tensor_scalar_mul(out=neg_mean[:, slots], in0=mean_var[:, slots, 0], scalar1=-1.0)
-            nc.gpsimd.tensor_scalar_add(out=var_eps[:, slots], in0=mean_var[:, slots, 1], scalar1=EPS)
-            nc.gpsimd.tensor_tensor(
-                out=rstd[:, slots], in0=var_eps[:, slots], in1=minus_half[:], op=ALU.pow
-            )
-            nc.gpsimd.tensor_tensor(
-                out=shift[:, slots], in0=neg_mean[:, slots], in1=rstd[:, slots], op=ALU.mult
-            )
-            for r in range(half * HALF, (half + 1) * HALF):
-                z = stage.tile([P, 2 * PASSES, 2, P], F32, bufs=3)
-                nc.scalar.activation(
-                    out=z[:],
-                    in_=x_sb[:, r, :].rearrange("p (c w e) -> p c e w", w=P, e=2),
-                    func=ACT.Identity,
-                    scale=rstd[:, r : r + 1],
-                    bias=shift[:, r : r + 1],
+        def statistics(r):
+            stats = small.tile([P, DIM // BN_WIDTH, 6], F32)
+            for s in range(DIM // BN_WIDTH):
+                nc.vector.bn_stats(
+                    out=stats[:, s, :], in_=x_sb[:, r, s * BN_WIDTH : (s + 1) * BN_WIDTH]
                 )
-                h_grouped = stage.tile([P, PASSES, P, PACK], BF16, align_bytes=64)
-                for g in range(PASSES):
-                    z_flip = flip_psum.tile([P, PACK, P], F32, tag="flip")
-                    for j in range(PACK):
-                        nc.tensor.transpose(z_flip[:, j, :], z[:, 2 * g + j // 2, j % 2, :], identity[:])
-                    nc.vector.tensor_tensor(
-                        out=h_grouped[:, g, :, :],
-                        in0=z_flip[:].rearrange("p j i -> p i j"),
-                        in1=gain[:, g, :].unsqueeze(1).to_broadcast([P, P, PACK]),
-                        op=ALU.mult,
-                    )
-                nc.vector.quantize_mx(
-                    out=h_codes[:, r, :, :].rearrange("p g i -> p (g i)").bitcast(FP8X4),
-                    scales=h_scales[:, r, :, :].rearrange("p g i -> p (g i)"),
-                    in_=h_grouped[:].rearrange("p g i j -> p (g i j)"),
-                )
+            nc.vector.bn_aggr(out=mean_var[:, r, :], in_=stats[:].rearrange("p s f -> p (s f)"))
+            one = slice(r, r + 1)
+            nc.gpsimd.tensor_scalar_add(out=var_eps[:, one], in0=mean_var[:, r, 1:2], scalar1=EPS)
+            nc.gpsimd.tensor_tensor(
+                out=rstd[:, one], in0=var_eps[:, one], in1=minus_half[:], op=ALU.pow
+            )
+            nc.gpsimd.tensor_scalar(
+                out=shift[:, one],
+                in0=mean_var[:, r, 0:1],
+                scalar1=rstd[:, one],
+                scalar2=-1.0,
+                op0=ALU.mult,
+                op1=ALU.mult,
+            )
 
-        def quantise_weights(c):
+        def normalise(r):
+            z = stage.tile([P, 2 * PASSES, 2, P], F32, name="z", bufs=4)
+            nc.scalar.activation(
+                out=z[:],
+                in_=x_sb[:, r, :].rearrange("p (c w e) -> p c e w", w=P, e=2),
+                func=ACT.Identity,
+                scale=rstd[:, r : r + 1],
+                bias=shift[:, r : r + 1],
+            )
+            z_tiles[r] = z
+
+        def flip_tokens(r):
+            z = z_tiles[r]
+            h_grouped = stage.tile([P, PASSES, P, PACK], BF16, name="h_grouped", align_bytes=64)
+            for g in range(PASSES):
+                z_flip = psum.tile([P, PACK, P], F32, tag="bank")
+                for j in range(PACK):
+                    nc.tensor.transpose(z_flip[:, j, :], z[:, 2 * g + j // 2, j % 2, :], identity[:])
+                nc.vector.tensor_tensor(
+                    out=h_grouped[:, g, :, :],
+                    in0=z_flip[:].rearrange("p j i -> p i j"),
+                    in1=gain[:, g, :].unsqueeze(1).to_broadcast([P, P, PACK]),
+                    op=ALU.mult,
+                )
+            h_grouped_tiles[r] = h_grouped
+
+        def quantise_tokens(r):
+            nc.vector.quantize_mx(
+                out=h_codes[:, r, :, :].rearrange("p g i -> p (g i)").bitcast(FP8X4),
+                scales=h_scales[:, r, :, :].rearrange("p g i -> p (g i)"),
+                in_=h_grouped_tiles[r][:].rearrange("p g i j -> p (g i j)"),
+            )
+
+        def flip_weights(c):
             words = w_raw[c][:].bitcast(F32)
-            w_grouped = stage.tile([P, PASSES, CHUNK, PACK], BF16, align_bytes=64)
+            w_grouped = stage.tile([P, PASSES, CHUNK, PACK], BF16, name="w_grouped", align_bytes=64)
             grouped_words = w_grouped[:].bitcast(F32)
             for g in range(PASSES):
                 for pair in range(ROW_BLOCKS // 2):
-                    w_flip = flip_psum.tile([P, 2, 2, P], F32, tag="flip")
+                    w_flip = psum.tile([P, 2, 2, P], F32, tag="bank")
                     for u in range(2):
                         for a in range(2):
                             first = (2 * g + u) * P
@@ -152,16 +176,19 @@ def tile_traceableencoderlayer_pa_kernel(tc, x, ln1_w, qkv_w, out_0, out_1, out_
                         out=grouped_words[:, g, 2 * pair * P : (2 * pair + 2) * P, :],
                         in_=w_flip[:].rearrange("p u a n -> p (a n) u"),
                     )
+            w_grouped_tiles[c] = w_grouped
+
+        def quantise_weights(c):
             nc.vector.quantize_mx(
                 out=w_codes[:, c, :, :].rearrange("p g n -> p (g n)").bitcast(FP8X4),
                 scales=w_scales[:, c, :, :].rearrange("p g n -> p (g n)"),
-                in_=w_grouped[:].rearrange("p g n j -> p (g n j)"),
+                in_=w_grouped_tiles[c][:].rearrange("p g n j -> p (g n j)"),
             )
 
         def project(c, first_slot, n_slots):
             result = res_pool.tile([P, CHUNK_HEADS, n_slots, HEAD_DIM], F32, tag="result")
             for r in range(first_slot, first_slot + n_slots):
-                acc = acc_psum.tile([P, CHUNK], F32)
+                acc = psum.tile([P, CHUNK], F32, tag="bank")
                 for g in range(PASSES):
                     nc.tensor.matmul_mx(
                         out=acc[:],
@@ -173,10 +200,10 @@ def tile_traceableencoderlayer_pa_kernel(tc, x, ln1_w, qkv_w, out_0, out_1, out_
                         stop=(g == PASSES - 1),
                     )
                 by_head = acc[:].rearrange("p (n d) -> p n d", d=HEAD_DIM)
-                if r % 2 == 1:
-                    nc.vector.tensor_copy(out=result[:, :, r - first_slot, :], in_=by_head)
-                else:
+                if r % 2 == 0:
                     nc.scalar.copy(out=result[:, :, r - first_slot, :], in_=by_head)
+                else:
+                    nc.vector.tensor_copy(out=result[:, :, r - first_slot, :], in_=by_head)
             which, first_head = divmod(c * CHUNK_HEADS, HEADS)
             for b in range(BATCH):
                 nc.sync.dma_start(
@@ -186,15 +213,38 @@ def tile_traceableencoderlayer_pa_kernel(tc, x, ln1_w, qkv_w, out_0, out_1, out_
                     in_=result[b:P:BATCH],
                 )
 
-        layer_norm_half(0)
+        for r in range(HALF):
+            statistics(r)
+            normalise(r)
+        widen_gain()
+        flip_tokens(0)
+        flip_tokens(1)
+        quantise_tokens(0)
+        flip_weights(0)
+        flip_tokens(2)
+        quantise_tokens(1)
+        flip_tokens(3)
+        quantise_tokens(2)
+        flip_weights(1)
+        quantise_tokens(3)
         quantise_weights(0)
-        for c in range(EARLY_CHUNKS):
-            quantise_weights(c + 1)
-            project(c, 0, HALF)
-        layer_norm_half(1)
+        statistics(HALF)
+        quantise_weights(1)
+        normalise(HALF)
+        statistics(HALF + 1)
+
+        for i in range(HALF):
+            if HALF + i + 1 < SLOTS:
+                normalise(HALF + i + 1)
+            project(i, 0, HALF)
+            if HALF + i + 2 < SLOTS:
+                statistics(HALF + i + 2)
+            flip_tokens(HALF + i)
+            flip_weights(i + 2)
+            quantise_tokens(HALF + i)
+            quantise_weights(i + 2)
+
         for c in range(EARLY_CHUNKS):
             project(c, HALF, HALF)
         for c in range(EARLY_CHUNKS, CHUNKS):
-            if c + 1 < CHUNKS:
-                quantise_weights(c + 1)
             project(c, 0, SLOTS)

@@ -218,20 +218,17 @@ def tile_traceableencoderlayer_pa_kernel(tc, x, ln1_w, qkv_w, out_0, out_1, out_
             normalise(r)
         widen_gain()
         flip_tokens(0)
-        flip_tokens(1)
-        quantise_tokens(0)
+        for r in range(1, HALF):
+            flip_tokens(r)
+            quantise_tokens(r - 1)
         flip_weights(0)
-        flip_tokens(2)
-        quantise_tokens(1)
-        flip_tokens(3)
-        quantise_tokens(2)
-        flip_weights(1)
-        quantise_tokens(3)
-        quantise_weights(0)
+        quantise_tokens(HALF - 1)
         statistics(HALF)
-        quantise_weights(1)
+        flip_weights(1)
+        quantise_weights(0)
         normalise(HALF)
         statistics(HALF + 1)
+        quantise_weights(1)
 
         for i in range(HALF):
             if HALF + i + 1 < SLOTS:

@@ -49,8 +49,8 @@ def tile_traceableencoderlayer_pa_kernel(tc, x, ln1_w, qkv_w, out_0, out_1, out_
         w_rows = qkv_w.rearrange("(c a p) k -> c p a k", a=ROW_BLOCKS, p=P)
         w_raw = []
 
-        def load_tokens(half):
-            slots = slice(half * HALF, (half + 1) * HALF)
+        def load_tokens(first_slot, n_slots):
+            slots = slice(first_slot, first_slot + n_slots)
             for b in range(BATCH):
                 nc.sync.dma_start(
                     out=x_sb[b:P:BATCH, slots, :],
@@ -62,9 +62,10 @@ def tile_traceableencoderlayer_pa_kernel(tc, x, ln1_w, qkv_w, out_0, out_1, out_
             nc.sync.dma_start(out=raw[:], in_=w_rows[c])
             w_raw.append(raw)
 
-        load_tokens(0)
+        load_tokens(0, 2)
+        load_tokens(2, 2)
         load_weights(0)
-        load_tokens(1)
+        load_tokens(HALF, HALF)
         for c in range(1, CHUNKS):
             load_weights(c)
 
@@ -231,13 +232,13 @@ def tile_traceableencoderlayer_pa_kernel(tc, x, ln1_w, qkv_w, out_0, out_1, out_
         quantise_weights(1)
 
         for i in range(HALF):
+            flip_weights(i + 2)
+            project(i, 0, HALF)
             if HALF + i + 1 < SLOTS:
                 normalise(HALF + i + 1)
-            project(i, 0, HALF)
             if HALF + i + 2 < SLOTS:
                 statistics(HALF + i + 2)
             flip_tokens(HALF + i)
-            flip_weights(i + 2)
             quantise_tokens(HALF + i)
             quantise_weights(i + 2)
 

@@ -65,16 +65,17 @@ def tile_traceableencoderlayer_pa_kernel(tc, x, ln1_w, qkv_w, out_0, out_1, out_
         load_tokens(0, 2)
         load_tokens(2, 2)
         load_weights(0)
-        load_tokens(HALF, HALF)
+        load_tokens(4, 2)
+        load_tokens(6, 2)
         for c in range(1, CHUNKS):
             load_weights(c)
 
         identity = keep.tile([P, P], F32)
         make_identity(nc, identity[:])
-        minus_half = keep.tile([P, 1], F32)
+        minus_half = keep.tile([P, 2], F32)
         nc.gpsimd.memset(minus_half[:], -0.5)
         table_warmer = keep.tile([P, 1], F32)
-        nc.scalar.activation(out=table_warmer[:], in_=minus_half[:], func=ACT.Identity)
+        nc.scalar.activation(out=table_warmer[:], in_=minus_half[:, 0:1], func=ACT.Identity)
 
         gain_rows = keep.tile([P, 2 * P], BF16)
         nc.vector.memset(gain_rows[:], 0.0)
@@ -93,6 +94,7 @@ def tile_traceableencoderlayer_pa_kernel(tc, x, ln1_w, qkv_w, out_0, out_1, out_
             )
 
         mean_var = keep.tile([P, SLOTS, 2], F32)
+        neg_mean = keep.tile([P, SLOTS], F32)
         var_eps = keep.tile([P, SLOTS], F32)
         rstd = keep.tile([P, SLOTS], F32)
         shift = keep.tile([P, SLOTS], F32)
@@ -104,25 +106,22 @@ def tile_traceableencoderlayer_pa_kernel(tc, x, ln1_w, qkv_w, out_0, out_1, out_
         h_grouped_tiles = {}
         w_grouped_tiles = {}
 
-        def statistics(r):
-            stats = small.tile([P, DIM // BN_WIDTH, 6], F32)
-            for s in range(DIM // BN_WIDTH):
-                nc.vector.bn_stats(
-                    out=stats[:, s, :], in_=x_sb[:, r, s * BN_WIDTH : (s + 1) * BN_WIDTH]
-                )
-            nc.vector.bn_aggr(out=mean_var[:, r, :], in_=stats[:].rearrange("p s f -> p (s f)"))
-            one = slice(r, r + 1)
-            nc.gpsimd.tensor_scalar_add(out=var_eps[:, one], in0=mean_var[:, r, 1:2], scalar1=EPS)
+        def statistics(first_slot):
+            pair = slice(first_slot, first_slot + 2)
+            for r in range(first_slot, first_slot + 2):
+                stats = small.tile([P, DIM // BN_WIDTH, 6], F32)
+                for s in range(DIM // BN_WIDTH):
+                    nc.vector.bn_stats(
+                        out=stats[:, s, :], in_=x_sb[:, r, s * BN_WIDTH : (s + 1) * BN_WIDTH]
+                    )
+                nc.vector.bn_aggr(out=mean_var[:, r, :], in_=stats[:].rearrange("p s f -> p (s f)"))
+            nc.vector.tensor_scalar_mul(out=neg_mean[:, pair], in0=mean_var[:, pair, 0], scalar1=-1.0)
+            nc.gpsimd.tensor_scalar_add(out=var_eps[:, pair], in0=mean_var[:, pair, 1], scalar1=EPS)
             nc.gpsimd.tensor_tensor(
-                out=rstd[:, one], in0=var_eps[:, one], in1=minus_half[:], op=ALU.pow
+                out=rstd[:, pair], in0=var_eps[:, pair], in1=minus_half[:], op=ALU.pow
             )
-            nc.gpsimd.tensor_scalar(
-                out=shift[:, one],
-                in0=mean_var[:, r, 0:1],
-                scalar1=rstd[:, one],
-                scalar2=-1.0,
-                op0=ALU.mult,
-                op1=ALU.mult,
+            nc.gpsimd.tensor_tensor(
+                out=shift[:, pair], in0=neg_mean[:, pair], in1=rstd[:, pair], op=ALU.mult
             )
 
         def normalise(r):
@@ -214,21 +213,22 @@ def tile_traceableencoderlayer_pa_kernel(tc, x, ln1_w, qkv_w, out_0, out_1, out_
                     in_=result[b:P:BATCH],
                 )
 
-        for r in range(HALF):
-            statistics(r)
-            normalise(r)
+        for first_slot in range(0, SLOTS, 2):
+            statistics(first_slot)
         widen_gain()
+        flip_weights(0)
+        for r in range(HALF):
+            normalise(r)
         flip_tokens(0)
-        for r in range(1, HALF):
+        flip_tokens(1)
+        quantise_tokens(0)
+        quantise_weights(0)
+        for r in range(2, HALF):
             flip_tokens(r)
             quantise_tokens(r - 1)
-        flip_weights(0)
         quantise_tokens(HALF - 1)
-        statistics(HALF)
         flip_weights(1)
-        quantise_weights(0)
         normalise(HALF)
-        statistics(HALF + 1)
         quantise_weights(1)
 
         for i in range(HALF):
@@ -236,8 +236,6 @@ def tile_traceableencoderlayer_pa_kernel(tc, x, ln1_w, qkv_w, out_0, out_1, out_
             project(i, 0, HALF)
             if HALF + i + 1 < SLOTS:
                 normalise(HALF + i + 1)
-            if HALF + i + 2 < SLOTS:
-                statistics(HALF + i + 2)
             flip_tokens(HALF + i)
             quantise_tokens(HALF + i)
             quantise_weights(i + 2)

@@ -206,7 +206,8 @@ def tile_traceableencoderlayer_pa_kernel(tc, x, ln1_w, qkv_w, out_0, out_1, out_
                     nc.vector.tensor_copy(out=result[:, :, r - first_slot, :], in_=by_head)
             which, first_head = divmod(c * CHUNK_HEADS, HEADS)
             for b in range(BATCH):
-                nc.sync.dma_start(
+                queue = nc.sync if b % 2 == 0 else nc.gpsimd
+                queue.dma_start(
                     out=outs[which][b, first_head : first_head + CHUNK_HEADS].rearrange(
                         "n (i r) d -> i n r d", r=SLOTS
                     )[:, :, first_slot : first_slot + n_slots, :],

from contextlib import ExitStack

import concourse.mybir as mybir
from concourse.masks import make_identity

F32 = mybir.dt.float32
BF16 = mybir.dt.bfloat16
U32 = mybir.dt.uint32
U8 = mybir.dt.uint8
FP8X4 = mybir.dt.float8_e4m3fn_x4
ALU = mybir.AluOpType
ACT = mybir.ActivationFunctionType

P = 128
BATCH, SEQ, DIM = 4, 256, 1024
HEADS, HEAD_DIM = 16, 64
EPS = 1e-5

PACK = 4
K_PASS = P * PACK
PASSES = DIM // K_PASS
SLOTS = BATCH * SEQ // P
HALF = SLOTS // 2
CHUNK = 512
CHUNK_HEADS = CHUNK // HEAD_DIM
CHUNKS = 3 * HEADS * HEAD_DIM // CHUNK
ROW_BLOCKS = CHUNK // P
BN_WIDTH = 512

EARLY_CHUNKS = HALF

FLOPS = 2 * BATCH * SEQ * DIM * 3 * HEADS * HEAD_DIM


def tile_traceableencoderlayer_pa_kernel(tc, x, ln1_w, qkv_w, out_0, out_1, out_2):
    nc = tc.nc
    outs = (out_0, out_1, out_2)

    with ExitStack() as ctx:
        keep = ctx.enter_context(tc.tile_pool(name="keep", bufs=1))
        small = ctx.enter_context(tc.tile_pool(name="small", bufs=4))
        stage = ctx.enter_context(tc.tile_pool(name="stage", bufs=2))
        w_pool = ctx.enter_context(tc.tile_pool(name="w_pool", bufs=CHUNKS))
        res_pool = ctx.enter_context(tc.tile_pool(name="res_pool", bufs=4))
        psum = ctx.enter_context(tc.psum_pool(name="psum", bufs=8))
        ctx.enter_context(tc.manual_schedule())

        x_sb = keep.tile([P, SLOTS, DIM], BF16)
        w_rows = qkv_w.rearrange("(c a p) k -> c p a k", a=ROW_BLOCKS, p=P)
        w_raw = []

        def load_tokens(first_slot, n_slots):
            slots = slice(first_slot, first_slot + n_slots)
            for b in range(BATCH):
                nc.sync.dma_start(
                    out=x_sb[b:P:BATCH, slots, :],
                    in_=x[b].rearrange("(i r) k -> i r k", r=SLOTS)[:, slots, :],
                )

        def load_weights(c):
            raw = w_pool.tile([P, ROW_BLOCKS, DIM], BF16, name="raw")
            nc.sync.dma_start(out=raw[:], in_=w_rows[c])
            w_raw.append(raw)

        load_tokens(0, 2)
        load_tokens(2, 2)
        load_weights(0)
        load_tokens(4, 2)
        load_tokens(6, 2)
        for c in range(1, CHUNKS):
            load_weights(c)

        identity = keep.tile([P, P], F32)
        make_identity(nc, identity[:])
        minus_half = keep.tile([P, 2], F32)
        nc.gpsimd.memset(minus_half[:], -0.5)
        table_warmer = keep.tile([P, 1], F32)
        nc.scalar.activation(out=table_warmer[:], in_=minus_half[:, 0:1], func=ACT.Identity)

        gain_rows = keep.tile([P, 2 * P], BF16)
        nc.vector.memset(gain_rows[:], 0.0)
        nc.scalar.dma_start(
            out=gain_rows[0 : 2 * PASSES, :], in_=ln1_w.rearrange("(r c) -> r c", c=2 * P)
        )
        gain_flip = psum.tile([P, PACK, P], F32, tag="bank")
        nc.tensor.transpose(gain_flip[:, 0, :], gain_rows[:].bitcast(F32), identity[:])
        gain_words = keep.tile([P, 2 * PASSES], F32)
        gain = keep.tile([P, PASSES, PACK], F32)

        def widen_gain():
            nc.vector.tensor_copy(out=gain_words[:], in_=gain_flip[:, 0, 0 : 2 * PASSES])
            nc.vector.tensor_copy(
                out=gain[:].rearrange("p g j -> p (g j)"), in_=gain_words[:].bitcast(BF16)
            )

        mean_var = keep.tile([P, SLOTS, 2], F32)
        neg_mean = keep.tile([P, SLOTS], F32)
        var_eps = keep.tile([P, SLOTS], F32)
        rstd = keep.tile([P, SLOTS], F32)
        shift = keep.tile([P, SLOTS], F32)
        h_codes = keep.tile([P, SLOTS, PASSES, P], U32, align_bytes=64)
        h_scales = keep.tile([P, SLOTS, PASSES, P], U8, align_bytes=64)
        w_codes = keep.tile([P, CHUNKS, PASSES, CHUNK], U32, align_bytes=64)
        w_scales = keep.tile([P, CHUNKS, PASSES, CHUNK], U8, align_bytes=64)
        z_tiles = {}
        h_grouped_tiles = {}
        w_grouped_tiles = {}

        def statistics(first_slot):
            pair = slice(first_slot, first_slot + 2)
            for r in range(first_slot, first_slot + 2):
                stats = small.tile([P, DIM // BN_WIDTH, 6], F32)
                for s in range(DIM // BN_WIDTH):
                    nc.vector.bn_stats(
                        out=stats[:, s, :], in_=x_sb[:, r, s * BN_WIDTH : (s + 1) * BN_WIDTH]
                    )
                nc.vector.bn_aggr(out=mean_var[:, r, :], in_=stats[:].rearrange("p s f -> p (s f)"))
            nc.vector.tensor_scalar_mul(out=neg_mean[:, pair], in0=mean_var[:, pair, 0], scalar1=-1.0)
            nc.gpsimd.tensor_scalar_add(out=var_eps[:, pair], in0=mean_var[:, pair, 1], scalar1=EPS)
            nc.gpsimd.tensor_tensor(
                out=rstd[:, pair], in0=var_eps[:, pair], in1=minus_half[:], op=ALU.pow
            )
            nc.gpsimd.tensor_tensor(
                out=shift[:, pair], in0=neg_mean[:, pair], in1=rstd[:, pair], op=ALU.mult
            )

        def normalise(r):
            z = stage.tile([P, 2 * PASSES, 2, P], F32, name="z", bufs=4)
            nc.scalar.activation(
                out=z[:],
                in_=x_sb[:, r, :].rearrange("p (c w e) -> p c e w", w=P, e=2),
                func=ACT.Identity,
                scale=rstd[:, r : r + 1],
                bias=shift[:, r : r + 1],
            )
            z_tiles[r] = z

        def flip_tokens(r):
            z = z_tiles[r]
            h_grouped = stage.tile([P, PASSES, P, PACK], BF16, name="h_grouped", align_bytes=64)
            for g in range(PASSES):
                z_flip = psum.tile([P, PACK, P], F32, tag="bank")
                for j in range(PACK):
                    nc.tensor.transpose(z_flip[:, j, :], z[:, 2 * g + j // 2, j % 2, :], identity[:])
                nc.vector.tensor_tensor(
                    out=h_grouped[:, g, :, :],
                    in0=z_flip[:].rearrange("p j i -> p i j"),
                    in1=gain[:, g, :].unsqueeze(1).to_broadcast([P, P, PACK]),
                    op=ALU.mult,
                )
            h_grouped_tiles[r] = h_grouped

        def quantise_tokens(r):
            nc.vector.quantize_mx(
                out=h_codes[:, r, :, :].rearrange("p g i -> p (g i)").bitcast(FP8X4),
                scales=h_scales[:, r, :, :].rearrange("p g i -> p (g i)"),
                in_=h_grouped_tiles[r][:].rearrange("p g i j -> p (g i j)"),
            )

        def flip_weights(c):
            words = w_raw[c][:].bitcast(F32)
            w_grouped = stage.tile([P, PASSES, CHUNK, PACK], BF16, name="w_grouped", align_bytes=64)
            grouped_words = w_grouped[:].bitcast(F32)
            for g in range(PASSES):
                for pair in range(ROW_BLOCKS // 2):
                    w_flip = psum.tile([P, 2, 2, P], F32, tag="bank")
                    for u in range(2):
                        for a in range(2):
                            first = (2 * g + u) * P
                            nc.tensor.transpose(
                                w_flip[:, u, a, :],
                                words[:, 2 * pair + a, first : first + P],
                                identity[:],
                            )
                    nc.scalar.copy(
                        out=grouped_words[:, g, 2 * pair * P : (2 * pair + 2) * P, :],
                        in_=w_flip[:].rearrange("p u a n -> p (a n) u"),
                    )
            w_grouped_tiles[c] = w_grouped

        def quantise_weights(c):
            nc.vector.quantize_mx(
                out=w_codes[:, c, :, :].rearrange("p g n -> p (g n)").bitcast(FP8X4),
                scales=w_scales[:, c, :, :].rearrange("p g n -> p (g n)"),
                in_=w_grouped_tiles[c][:].rearrange("p g n j -> p (g n j)"),
            )

        def project(c, first_slot, n_slots):
            result = res_pool.tile([P, CHUNK_HEADS, n_slots, HEAD_DIM], F32, tag="result")
            for r in range(first_slot, first_slot + n_slots):
                acc = psum.tile([P, CHUNK], F32, tag="bank")
                for g in range(PASSES):
                    nc.tensor.matmul_mx(
                        out=acc[:],
                        lhsT=h_codes[:, r, g, :].bitcast(FP8X4),
                        lhsT_scale=h_scales[:, r, g, :],
                        rhs=w_codes[:, c, g, :].bitcast(FP8X4),
                        rhs_scale=w_scales[:, c, g, :],
                        start=(g == 0),
                        stop=(g == PASSES - 1),
                    )
                by_head = acc[:].rearrange("p (n d) -> p n d", d=HEAD_DIM)
                if r % 2 == 0:
                    nc.scalar.copy(out=result[:, :, r - first_slot, :], in_=by_head)
                else:
                    nc.vector.tensor_copy(out=result[:, :, r - first_slot, :], in_=by_head)
            which, first_head = divmod(c * CHUNK_HEADS, HEADS)
            for b in range(BATCH):
                queue = nc.sync if b % 2 == 0 else nc.gpsimd
                queue.dma_start(
                    out=outs[which][b, first_head : first_head + CHUNK_HEADS].rearrange(
                        "n (i r) d -> i n r d", r=SLOTS
                    )[:, :, first_slot : first_slot + n_slots, :],
                    in_=result[b:P:BATCH],
                )

        for first_slot in range(0, SLOTS, 2):
            statistics(first_slot)
        widen_gain()
        flip_weights(0)
        for r in range(HALF):
            normalise(r)
        flip_tokens(0)
        flip_tokens(1)
        quantise_tokens(0)
        quantise_weights(0)
        for r in range(2, HALF):
            flip_tokens(r)
            quantise_tokens(r - 1)
        quantise_tokens(HALF - 1)
        flip_weights(1)
        normalise(HALF)
        quantise_weights(1)

        for i in range(HALF):
            flip_weights(i + 2)
            project(i, 0, HALF)
            if HALF + i + 1 < SLOTS:
                normalise(HALF + i + 1)
            flip_tokens(HALF + i)
            quantise_tokens(HALF + i)
            quantise_weights(i + 2)

        for c in range(EARLY_CHUNKS):
            project(c, HALF, HALF)
        for c in range(EARLY_CHUNKS, CHUNKS):
            project(c, 0, SLOTS)
